import numpy as np
import ml_dtypes

BF16 = ml_dtypes.bfloat16


def bf(x):
    return np.asarray(x, np.float32).astype(BF16)


def f32(x):
    return np.asarray(x, np.float32)


def f64(x):
    return np.asarray(x).astype(np.float64)


def striped(idx):
    return np.tile(idx.reshape(-1, 16).T, (8, 1))


D, S, M1, M2, K, T, N = 128, 512, 256, 256, 2, 128, 256


def setup_inputs():
    return {
        "table": bf(np.random.standard_normal((D, S))),
        "w1": bf(np.random.standard_normal((D, M1)) / np.sqrt(D)),
        "b1": f32(0.1 * np.random.standard_normal((M1, 1))),
        "w2": bf(np.random.standard_normal((M1, M2)) / np.sqrt(M1)),
        "b2": f32(0.1 * np.random.standard_normal((M2, 1))),
        "offs": striped(np.random.permutation(np.tile(np.arange(S), 2))[:N]),
    }


def reference(table, w1, b1, w2, b2, offs):
    idx = offs[:16].T.reshape(-1)
    y = f64(w1).T @ f64(table)[:, idx]
    h = np.maximum(y.reshape(M1, K, T).sum(axis=1) / K + f64(b1), 0.0)
    return np.maximum(f64(w2).T @ h + f64(b2), 0.0)

@@ -1,0 +1,72 @@
+import concourse.mybir as mybir
+
+P = 128
+NODES = 512
+TARGETS = 128
+NEIGHBOURS = 2
+HIDDEN = 256
+OUTPUTS = 256
+HIDDEN_BLOCKS = HIDDEN // P
+OUTPUT_BLOCKS = OUTPUTS // P
+LIST = NEIGHBOURS * TARGETS
+OFFSETS_IN_A_COLUMN = 16
+COLUMNS_OF_A_NEIGHBOUR = TARGETS // OFFSETS_IN_A_COLUMN
+
+FLOPS = 2 * P * HIDDEN * LIST + 2 * HIDDEN * OUTPUTS * TARGETS
+
+BF16 = mybir.dt.bfloat16
+F32 = mybir.dt.float32
+U16 = mybir.dt.uint16
+RELU = mybir.ActivationFunctionType.Relu
+
+
+def tile_hot_gnn_kernel(tc, table, w1, b1, w2, b2, offs, out):
+    nc = tc.nc
+    with (
+        tc.tile_pool(name="held", bufs=1) as held,
+        tc.psum_pool(name="psum", bufs=1) as psum,
+    ):
+        offsets = held.tile([P, LIST // OFFSETS_IN_A_COLUMN], U16, name="offsets")
+        nc.sync.dma_start(offsets[:], offs)
+        nodes = held.tile([P, NODES], BF16, name="nodes")
+        nc.sync.dma_start(nodes[:], table)
+        w1_sb = held.tile([P, HIDDEN], BF16, name="w1_sb")
+        nc.scalar.dma_start(w1_sb[:], w1)
+        bias1 = [held.tile([P, 1], F32, name=f"bias1_{m}") for m in range(HIDDEN_BLOCKS)]
+        for m in range(HIDDEN_BLOCKS):
+            nc.scalar.dma_start(bias1[m][:], b1[m * P : (m + 1) * P, :])
+        w2_sb = held.tile([P, HIDDEN_BLOCKS, OUTPUTS], BF16, name="w2_sb")
+        nc.gpsimd.dma_start(w2_sb[:], w2.rearrange("(m p) q -> p m q", p=P))
+        bias2 = [held.tile([P, 1], F32, name=f"bias2_{q}") for q in range(OUTPUT_BLOCKS)]
+        for q in range(OUTPUT_BLOCKS):
+            nc.gpsimd.dma_start(bias2[q][:], b2[q * P : (q + 1) * P, :])
+
+        hidden = []
+        for m in range(HIDDEN_BLOCKS):
+            summed = psum.tile([P, TARGETS], F32, name=f"summed{m}")
+            for k in range(NEIGHBOURS):
+                neighbour_k = offsets[:, k * COLUMNS_OF_A_NEIGHBOUR : (k + 1) * COLUMNS_OF_A_NEIGHBOUR]
+                nc.tensor.matmul(
+                    summed[:],
+                    w1_sb[:, m * P : (m + 1) * P],
+                    nodes[:].indirect(neighbour_k),
+                    start=(k == 0),
+                    stop=(k == NEIGHBOURS - 1),
+                )
+            h = held.tile([P, TARGETS], BF16, name=f"h{m}")
+            nc.scalar.activation(h[:], summed[:], RELU, bias=bias1[m][:], scale=1.0 / NEIGHBOURS)
+            hidden.append(h)
+
+        for q in range(OUTPUT_BLOCKS):
+            projected = psum.tile([P, TARGETS], F32, name=f"projected{q}")
+            for m in range(HIDDEN_BLOCKS):
+                nc.tensor.matmul(
+                    projected[:],
+                    w2_sb[:, m, q * P : (q + 1) * P],
+                    hidden[m][:],
+                    start=(m == 0),
+                    stop=(m == HIDDEN_BLOCKS - 1),
+                )
+            result = held.tile([P, TARGETS], F32, name=f"result{q}")
+            nc.scalar.activation(result[:], projected[:], RELU, bias=bias2[q][:], scale=1.0)
+            nc.sync.dma_start(out[q * P : (q + 1) * P, :], result[:])

@@ -32,14 +32,17 @@ def tile_hot_gnn_kernel(tc, table, w1, b1, w2, b2, offs, out):
         nc.sync.dma_start(nodes[:], table)
         w1_sb = held.tile([P, HIDDEN], BF16, name="w1_sb")
         nc.scalar.dma_start(w1_sb[:], w1)
-        bias1 = [held.tile([P, 1], F32, name=f"bias1_{m}") for m in range(HIDDEN_BLOCKS)]
-        for m in range(HIDDEN_BLOCKS):
-            nc.scalar.dma_start(bias1[m][:], b1[m * P : (m + 1) * P, :])
+        bias1 = held.tile([P, HIDDEN_BLOCKS], F32, name="bias1")
+        bias2 = held.tile([P, OUTPUT_BLOCKS], F32, name="bias2")
+        with nc.allow_non_contiguous_dma(reason="a bias is spread one element to a partition"):
+            nc.scalar.dma_start(bias1[:], b1.rearrange("(m p) one -> p (m one)", p=P))
+            nc.scalar.dma_start(bias2[:], b2.rearrange("(q p) one -> p (q one)", p=P))
         w2_sb = held.tile([P, HIDDEN_BLOCKS, OUTPUTS], BF16, name="w2_sb")
-        nc.gpsimd.dma_start(w2_sb[:], w2.rearrange("(m p) q -> p m q", p=P))
-        bias2 = [held.tile([P, 1], F32, name=f"bias2_{q}") for q in range(OUTPUT_BLOCKS)]
-        for q in range(OUTPUT_BLOCKS):
-            nc.gpsimd.dma_start(bias2[q][:], b2[q * P : (q + 1) * P, :])
+        nc.sync.dma_start(w2_sb[:], w2.rearrange("(m p) q -> p m q", p=P))
+
+        scratch = held.tile([P, 1], F32, name="scratch")
+        nc.vector.memset(scratch[:], 0.0)
+        nc.scalar.activation(scratch[:], scratch[:], RELU)
 
         hidden = []
         for m in range(HIDDEN_BLOCKS):
@@ -54,7 +57,7 @@ def tile_hot_gnn_kernel(tc, table, w1, b1, w2, b2, offs, out):
                     stop=(k == NEIGHBOURS - 1),
                 )
             h = held.tile([P, TARGETS], BF16, name=f"h{m}")
-            nc.scalar.activation(h[:], summed[:], RELU, bias=bias1[m][:], scale=1.0 / NEIGHBOURS)
+            nc.scalar.activation(h[:], summed[:], RELU, bias=bias1[:, m : m + 1], scale=1.0 / NEIGHBOURS)
             hidden.append(h)
 
         for q in range(OUTPUT_BLOCKS):
@@ -68,5 +71,5 @@ def tile_hot_gnn_kernel(tc, table, w1, b1, w2, b2, offs, out):
                     stop=(m == HIDDEN_BLOCKS - 1),
                 )
             result = held.tile([P, TARGETS], F32, name=f"result{q}")
-            nc.scalar.activation(result[:], projected[:], RELU, bias=bias2[q][:], scale=1.0)
+            nc.scalar.activation(result[:], projected[:], RELU, bias=bias2[:, q : q + 1], scale=1.0)
             nc.sync.dma_start(out[q * P : (q + 1) * P, :], result[:])

@@ -18,6 +18,8 @@ BF16 = mybir.dt.bfloat16
 F32 = mybir.dt.float32
 U16 = mybir.dt.uint16
 RELU = mybir.ActivationFunctionType.Relu
+ADD = mybir.AluOpType.add
+MAX = mybir.AluOpType.max
 
 
 def tile_hot_gnn_kernel(tc, table, w1, b1, w2, b2, offs, out):
@@ -60,16 +62,21 @@ def tile_hot_gnn_kernel(tc, table, w1, b1, w2, b2, offs, out):
             nc.scalar.activation(h[:], summed[:], RELU, bias=bias1[:, m : m + 1], scale=1.0 / NEIGHBOURS)
             hidden.append(h)
 
-        for q in range(OUTPUT_BLOCKS):
-            projected = psum.tile([P, TARGETS], F32, name=f"projected{q}")
-            for m in range(HIDDEN_BLOCKS):
+        projected = [psum.tile([P, TARGETS], F32, name=f"projected{q}") for q in range(OUTPUT_BLOCKS)]
+        for m in range(HIDDEN_BLOCKS):
+            for q in range(OUTPUT_BLOCKS):
                 nc.tensor.matmul(
-                    projected[:],
+                    projected[q][:],
                     w2_sb[:, m, q * P : (q + 1) * P],
                     hidden[m][:],
                     start=(m == 0),
                     stop=(m == HIDDEN_BLOCKS - 1),
                 )
+        for q in range(OUTPUT_BLOCKS):
             result = held.tile([P, TARGETS], F32, name=f"result{q}")
-            nc.scalar.activation(result[:], projected[:], RELU, bias=bias2[:, q : q + 1], scale=1.0)
-            nc.sync.dma_start(out[q * P : (q + 1) * P, :], result[:])
+            if q % 2 == 0:
+                nc.scalar.activation(result[:], projected[q][:], RELU, bias=bias2[:, q : q + 1], scale=1.0)
+                nc.sync.dma_start(out[q * P : (q + 1) * P, :], result[:])
+            else:
+                nc.vector.tensor_scalar(result[:], projected[q][:], bias2[:, q : q + 1], 0.0, ADD, MAX)
+                nc.scalar.dma_start(out[q * P : (q + 1) * P, :], result[:])

@@ -11,6 +11,7 @@ OUTPUT_BLOCKS = OUTPUTS // P
 LIST = NEIGHBOURS * TARGETS
 OFFSETS_IN_A_COLUMN = 16
 COLUMNS_OF_A_NEIGHBOUR = TARGETS // OFFSETS_IN_A_COLUMN
+WARM_UP = 14
 
 FLOPS = 2 * P * HIDDEN * LIST + 2 * HIDDEN * OUTPUTS * TARGETS
 
@@ -42,9 +43,13 @@ def tile_hot_gnn_kernel(tc, table, w1, b1, w2, b2, offs, out):
         w2_sb = held.tile([P, HIDDEN_BLOCKS, OUTPUTS], BF16, name="w2_sb")
         nc.sync.dma_start(w2_sb[:], w2.rearrange("(m p) q -> p m q", p=P))
 
+        zeros = held.tile([P, P], BF16, name="zeros")
+        nc.vector.memset(zeros[:], 0.0)
         scratch = held.tile([P, 1], F32, name="scratch")
-        nc.vector.memset(scratch[:], 0.0)
-        nc.scalar.activation(scratch[:], scratch[:], RELU)
+        nc.scalar.activation(scratch[:], zeros[:, 0:1], RELU)
+        unused = psum.tile([P, P], F32, name="unused")
+        for i in range(WARM_UP):
+            nc.tensor.matmul(unused[:], zeros[:], zeros[:], start=True, stop=True)
 
         hidden = []
         for m in range(HIDDEN_BLOCKS):

@@ -32,9 +32,9 @@ def tile_hot_gnn_kernel(tc, table, w1, b1, w2, b2, offs, out):
         offsets = held.tile([P, LIST // OFFSETS_IN_A_COLUMN], U16, name="offsets")
         nc.sync.dma_start(offsets[:], offs)
         nodes = held.tile([P, NODES], BF16, name="nodes")
-        nc.sync.dma_start(nodes[:], table)
+        nc.scalar.dma_start(nodes[:], table)
         w1_sb = held.tile([P, HIDDEN], BF16, name="w1_sb")
-        nc.scalar.dma_start(w1_sb[:], w1)
+        nc.sync.dma_start(w1_sb[:], w1)
         bias1 = held.tile([P, HIDDEN_BLOCKS], F32, name="bias1")
         bias2 = held.tile([P, OUTPUT_BLOCKS], F32, name="bias2")
         with nc.allow_non_contiguous_dma(reason="a bias is spread one element to a partition"):

@@ -37,11 +37,10 @@ def tile_hot_gnn_kernel(tc, table, w1, b1, w2, b2, offs, out):
         nc.sync.dma_start(w1_sb[:], w1)
         bias1 = held.tile([P, HIDDEN_BLOCKS], F32, name="bias1")
         bias2 = held.tile([P, OUTPUT_BLOCKS], F32, name="bias2")
-        with nc.allow_non_contiguous_dma(reason="a bias is spread one element to a partition"):
-            nc.scalar.dma_start(bias1[:], b1.rearrange("(m p) one -> p (m one)", p=P))
-            nc.scalar.dma_start(bias2[:], b2.rearrange("(q p) one -> p (q one)", p=P))
+        nc.scalar.dma_start(bias1[:], b1.rearrange("(p m) one -> p (m one)", p=P))
+        nc.scalar.dma_start(bias2[:], b2.rearrange("(p q) one -> p (q one)", p=P))
         w2_sb = held.tile([P, HIDDEN_BLOCKS, OUTPUTS], BF16, name="w2_sb")
-        nc.sync.dma_start(w2_sb[:], w2.rearrange("(m p) q -> p m q", p=P))
+        nc.sync.dma_start(w2_sb[:], w2.rearrange("(p m) q -> p m q", p=P))
 
         zeros = held.tile([P, P], BF16, name="zeros")
         nc.vector.memset(zeros[:], 0.0)
@@ -58,7 +57,7 @@ def tile_hot_gnn_kernel(tc, table, w1, b1, w2, b2, offs, out):
                 neighbour_k = offsets[:, k * COLUMNS_OF_A_NEIGHBOUR : (k + 1) * COLUMNS_OF_A_NEIGHBOUR]
                 nc.tensor.matmul(
                     summed[:],
-                    w1_sb[:, m * P : (m + 1) * P],
+                    w1_sb[:, m::HIDDEN_BLOCKS],
                     nodes[:].indirect(neighbour_k),
                     start=(k == 0),
                     stop=(k == NEIGHBOURS - 1),
@@ -72,16 +71,17 @@ def tile_hot_gnn_kernel(tc, table, w1, b1, w2, b2, offs, out):
             for q in range(OUTPUT_BLOCKS):
                 nc.tensor.matmul(
                     projected[q][:],
-                    w2_sb[:, m, q * P : (q + 1) * P],
+                    w2_sb[:, m, q::OUTPUT_BLOCKS],
                     hidden[m][:],
                     start=(m == 0),
                     stop=(m == HIDDEN_BLOCKS - 1),
                 )
+        rows = out.rearrange("(p q) t -> p q t", q=OUTPUT_BLOCKS)
         for q in range(OUTPUT_BLOCKS):
             result = held.tile([P, TARGETS], F32, name=f"result{q}")
             if q % 2 == 0:
                 nc.scalar.activation(result[:], projected[q][:], RELU, bias=bias2[:, q : q + 1], scale=1.0)
-                nc.sync.dma_start(out[q * P : (q + 1) * P, :], result[:])
+                nc.sync.dma_start(rows[:, q, :], result[:])
             else:
                 nc.vector.tensor_scalar(result[:], projected[q][:], bias2[:, q : q + 1], 0.0, ADD, MAX)
-                nc.scalar.dma_start(out[q * P : (q + 1) * P, :], result[:])
+                nc.scalar.dma_start(rows[:, q, :], result[:])

@@ -21,6 +21,7 @@ U16 = mybir.dt.uint16
 RELU = mybir.ActivationFunctionType.Relu
 ADD = mybir.AluOpType.add
 MAX = mybir.AluOpType.max
+MULT = mybir.AluOpType.mult
 
 
 def tile_hot_gnn_kernel(tc, table, w1, b1, w2, b2, offs, out):
@@ -50,6 +51,10 @@ def tile_hot_gnn_kernel(tc, table, w1, b1, w2, b2, offs, out):
         for i in range(WARM_UP):
             nc.tensor.matmul(unused[:], zeros[:], zeros[:], start=True, stop=True)
 
+        last = HIDDEN_BLOCKS - 1
+        w1_halved = held.tile([P, P], BF16, name="w1_halved")
+        nc.vector.tensor_scalar(w1_halved[:], w1_sb[:, last::HIDDEN_BLOCKS], 1.0 / NEIGHBOURS, None, MULT)
+
         hidden = []
         for m in range(HIDDEN_BLOCKS):
             summed = psum.tile([P, TARGETS], F32, name=f"summed{m}")
@@ -57,13 +62,16 @@ def tile_hot_gnn_kernel(tc, table, w1, b1, w2, b2, offs, out):
                 neighbour_k = offsets[:, k * COLUMNS_OF_A_NEIGHBOUR : (k + 1) * COLUMNS_OF_A_NEIGHBOUR]
                 nc.tensor.matmul(
                     summed[:],
-                    w1_sb[:, m::HIDDEN_BLOCKS],
+                    w1_halved[:] if m == last else w1_sb[:, m::HIDDEN_BLOCKS],
                     nodes[:].indirect(neighbour_k),
                     start=(k == 0),
                     stop=(k == NEIGHBOURS - 1),
                 )
             h = held.tile([P, TARGETS], BF16, name=f"h{m}")
-            nc.scalar.activation(h[:], summed[:], RELU, bias=bias1[:, m : m + 1], scale=1.0 / NEIGHBOURS)
+            if m == last:
+                nc.vector.tensor_scalar(h[:], summed[:], bias1[:, m : m + 1], 0.0, ADD, MAX)
+            else:
+                nc.scalar.activation(h[:], summed[:], RELU, bias=bias1[:, m : m + 1], scale=1.0 / NEIGHBOURS)
             hidden.append(h)
 
         projected = [psum.tile([P, TARGETS], F32, name=f"projected{q}") for q in range(OUTPUT_BLOCKS)]

@@ -11,6 +11,8 @@ OUTPUT_BLOCKS = OUTPUTS // P
 LIST = NEIGHBOURS * TARGETS
 OFFSETS_IN_A_COLUMN = 16
 COLUMNS_OF_A_NEIGHBOUR = TARGETS // OFFSETS_IN_A_COLUMN
+HALVES = 2
+HALF = TARGETS // HALVES
 WARM_UP = 14
 
 FLOPS = 2 * P * HIDDEN * LIST + 2 * HIDDEN * OUTPUTS * TARGETS
@@ -55,41 +57,45 @@ def tile_hot_gnn_kernel(tc, table, w1, b1, w2, b2, offs, out):
         w1_halved = held.tile([P, P], BF16, name="w1_halved")
         nc.vector.tensor_scalar(w1_halved[:], w1_sb[:, last::HIDDEN_BLOCKS], 1.0 / NEIGHBOURS, None, MULT)
 
-        hidden = []
+        summed = [psum.tile([P, TARGETS], F32, name=f"summed{m}") for m in range(HIDDEN_BLOCKS)]
         for m in range(HIDDEN_BLOCKS):
-            summed = psum.tile([P, TARGETS], F32, name=f"summed{m}")
             for k in range(NEIGHBOURS):
                 neighbour_k = offsets[:, k * COLUMNS_OF_A_NEIGHBOUR : (k + 1) * COLUMNS_OF_A_NEIGHBOUR]
                 nc.tensor.matmul(
-                    summed[:],
+                    summed[m][:],
                     w1_halved[:] if m == last else w1_sb[:, m::HIDDEN_BLOCKS],
                     nodes[:].indirect(neighbour_k),
                     start=(k == 0),
                     stop=(k == NEIGHBOURS - 1),
                 )
-            h = held.tile([P, TARGETS], BF16, name=f"h{m}")
-            if m == last:
-                nc.vector.tensor_scalar(h[:], summed[:], bias1[:, m : m + 1], 0.0, ADD, MAX)
-            else:
-                nc.scalar.activation(h[:], summed[:], RELU, bias=bias1[:, m : m + 1], scale=1.0 / NEIGHBOURS)
-            hidden.append(h)
-
-        projected = [psum.tile([P, TARGETS], F32, name=f"projected{q}") for q in range(OUTPUT_BLOCKS)]
+        hidden = [[held.tile([P, HALF], BF16, name=f"h{m}_{s}") for s in range(HALVES)] for m in range(HIDDEN_BLOCKS)]
         for m in range(HIDDEN_BLOCKS):
+            for s in range(HALVES):
+                of_half = summed[m][:, s * HALF : (s + 1) * HALF]
+                if m == last:
+                    nc.vector.tensor_scalar(hidden[m][s][:], of_half, bias1[:, m : m + 1], 0.0, ADD, MAX)
+                else:
+                    nc.scalar.activation(hidden[m][s][:], of_half, RELU, bias=bias1[:, m : m + 1], scale=1.0 / NEIGHBOURS)
+
+        results = [held.tile([P, TARGETS], F32, name=f"result{q}") for q in range(OUTPUT_BLOCKS)]
+        for s in range(HALVES):
+            half = slice(s * HALF, (s + 1) * HALF)
+            projected = [psum.tile([P, HALF], F32, name=f"projected{s}_{q}") for q in range(OUTPUT_BLOCKS)]
+            for m in range(HIDDEN_BLOCKS):
+                for q in range(OUTPUT_BLOCKS):
+                    nc.tensor.matmul(
+                        projected[q][:],
+                        w2_sb[:, m, q::OUTPUT_BLOCKS],
+                        hidden[m][s][:],
+                        start=(m == 0),
+                        stop=(m == HIDDEN_BLOCKS - 1),
+                    )
             for q in range(OUTPUT_BLOCKS):
-                nc.tensor.matmul(
-                    projected[q][:],
-                    w2_sb[:, m, q::OUTPUT_BLOCKS],
-                    hidden[m][:],
-                    start=(m == 0),
-                    stop=(m == HIDDEN_BLOCKS - 1),
-                )
+                if q % 2 == 0:
+                    nc.scalar.activation(results[q][:, half], projected[q][:], RELU, bias=bias2[:, q : q + 1], scale=1.0)
+                else:
+                    nc.vector.tensor_scalar(results[q][:, half], projected[q][:], bias2[:, q : q + 1], 0.0, ADD, MAX)
         rows = out.rearrange("(p q) t -> p q t", q=OUTPUT_BLOCKS)
         for q in range(OUTPUT_BLOCKS):
-            result = held.tile([P, TARGETS], F32, name=f"result{q}")
-            if q % 2 == 0:
-                nc.scalar.activation(result[:], projected[q][:], RELU, bias=bias2[:, q : q + 1], scale=1.0)
-                nc.sync.dma_start(rows[:, q, :], result[:])
-            else:
-                nc.vector.tensor_scalar(result[:], projected[q][:], bias2[:, q : q + 1], 0.0, ADD, MAX)
-                nc.scalar.dma_start(rows[:, q, :], result[:])
+            queue = nc.sync if q % 2 == 0 else nc.scalar
+            queue.dma_start(rows[:, q, :], results[q][:])

import concourse.mybir as mybir

P = 128
NODES = 512
TARGETS = 128
NEIGHBOURS = 2
HIDDEN = 256
OUTPUTS = 256
HIDDEN_BLOCKS = HIDDEN // P
OUTPUT_BLOCKS = OUTPUTS // P
LIST = NEIGHBOURS * TARGETS
OFFSETS_IN_A_COLUMN = 16
COLUMNS_OF_A_NEIGHBOUR = TARGETS // OFFSETS_IN_A_COLUMN
HALVES = 2
HALF = TARGETS // HALVES
WARM_UP = 14

FLOPS = 2 * P * HIDDEN * LIST + 2 * HIDDEN * OUTPUTS * TARGETS

BF16 = mybir.dt.bfloat16
F32 = mybir.dt.float32
U16 = mybir.dt.uint16
RELU = mybir.ActivationFunctionType.Relu
ADD = mybir.AluOpType.add
MAX = mybir.AluOpType.max
MULT = mybir.AluOpType.mult


def tile_hot_gnn_kernel(tc, table, w1, b1, w2, b2, offs, out):
    nc = tc.nc
    with (
        tc.tile_pool(name="held", bufs=1) as held,
        tc.psum_pool(name="psum", bufs=1) as psum,
    ):
        offsets = held.tile([P, LIST // OFFSETS_IN_A_COLUMN], U16, name="offsets")
        nc.sync.dma_start(offsets[:], offs)
        nodes = held.tile([P, NODES], BF16, name="nodes")
        nc.scalar.dma_start(nodes[:], table)
        w1_sb = held.tile([P, HIDDEN], BF16, name="w1_sb")
        nc.sync.dma_start(w1_sb[:], w1)
        bias1 = held.tile([P, HIDDEN_BLOCKS], F32, name="bias1")
        bias2 = held.tile([P, OUTPUT_BLOCKS], F32, name="bias2")
        nc.scalar.dma_start(bias1[:], b1.rearrange("(p m) one -> p (m one)", p=P))
        nc.scalar.dma_start(bias2[:], b2.rearrange("(p q) one -> p (q one)", p=P))
        w2_sb = held.tile([P, HIDDEN_BLOCKS, OUTPUTS], BF16, name="w2_sb")
        nc.sync.dma_start(w2_sb[:], w2.rearrange("(p m) q -> p m q", p=P))

        zeros = held.tile([P, P], BF16, name="zeros")
        nc.vector.memset(zeros[:], 0.0)
        scratch = held.tile([P, 1], F32, name="scratch")
        nc.scalar.activation(scratch[:], zeros[:, 0:1], RELU)
        unused = psum.tile([P, P], F32, name="unused")
        for i in range(WARM_UP):
            nc.tensor.matmul(unused[:], zeros[:], zeros[:], start=True, stop=True)

        last = HIDDEN_BLOCKS - 1
        w1_halved = held.tile([P, P], BF16, name="w1_halved")
        nc.vector.tensor_scalar(w1_halved[:], w1_sb[:, last::HIDDEN_BLOCKS], 1.0 / NEIGHBOURS, None, MULT)

        summed = [psum.tile([P, TARGETS], F32, name=f"summed{m}") for m in range(HIDDEN_BLOCKS)]
        for m in range(HIDDEN_BLOCKS):
            for k in range(NEIGHBOURS):
                neighbour_k = offsets[:, k * COLUMNS_OF_A_NEIGHBOUR : (k + 1) * COLUMNS_OF_A_NEIGHBOUR]
                nc.tensor.matmul(
                    summed[m][:],
                    w1_halved[:] if m == last else w1_sb[:, m::HIDDEN_BLOCKS],
                    nodes[:].indirect(neighbour_k),
                    start=(k == 0),
                    stop=(k == NEIGHBOURS - 1),
                )
        hidden = [[held.tile([P, HALF], BF16, name=f"h{m}_{s}") for s in range(HALVES)] for m in range(HIDDEN_BLOCKS)]
        for m in range(HIDDEN_BLOCKS):
            for s in range(HALVES):
                of_half = summed[m][:, s * HALF : (s + 1) * HALF]
                if m == last:
                    nc.vector.tensor_scalar(hidden[m][s][:], of_half, bias1[:, m : m + 1], 0.0, ADD, MAX)
                else:
                    nc.scalar.activation(hidden[m][s][:], of_half, RELU, bias=bias1[:, m : m + 1], scale=1.0 / NEIGHBOURS)

        results = [held.tile([P, TARGETS], F32, name=f"result{q}") for q in range(OUTPUT_BLOCKS)]
        for s in range(HALVES):
            half = slice(s * HALF, (s + 1) * HALF)
            projected = [psum.tile([P, HALF], F32, name=f"projected{s}_{q}") for q in range(OUTPUT_BLOCKS)]
            for m in range(HIDDEN_BLOCKS):
                for q in range(OUTPUT_BLOCKS):
                    nc.tensor.matmul(
                        projected[q][:],
                        w2_sb[:, m, q::OUTPUT_BLOCKS],
                        hidden[m][s][:],
                        start=(m == 0),
                        stop=(m == HIDDEN_BLOCKS - 1),
                    )
            for q in range(OUTPUT_BLOCKS):
                if q % 2 == 0:
                    nc.scalar.activation(results[q][:, half], projected[q][:], RELU, bias=bias2[:, q : q + 1], scale=1.0)
                else:
                    nc.vector.tensor_scalar(results[q][:, half], projected[q][:], bias2[:, q : q + 1], 0.0, ADD, MAX)
        rows = out.rearrange("(p q) t -> p q t", q=OUTPUT_BLOCKS)
        for q in range(OUTPUT_BLOCKS):
            queue = nc.sync if q % 2 == 0 else nc.scalar
            queue.dma_start(rows[:, q, :], results[q][:])
